import numpy as np
import ml_dtypes

BF16 = ml_dtypes.bfloat16


def bf(x):
    return np.asarray(x, np.float32).astype(BF16)


def f32(x):
    return np.asarray(x, np.float32)


def f64(x):
    return np.asarray(x).astype(np.float64)


def striped(idx):
    return np.tile(idx.reshape(-1, 16).T, (8, 1))


C, S, B, H, N = 512, 512, 4, 256, 1024
MAXD, LO = 2.0, 0.25


def setup_inputs():
    u = np.random.uniform(size=(C, S))
    q = np.random.uniform(size=(C, B))
    dis = f32(LO + (MAXD - LO) * (u / u.max()))
    prob = f32((q - q.min()) / (q.max() - q.min()))
    idx = np.concatenate([np.random.permutation(S)[:H] for _ in range(B)])
    return {"dis": dis, "prob": prob, "offs": striped(idx)}


def reference(dis, prob, offs):
    idx = offs[:16].T.reshape(-1)
    p = np.repeat(f64(prob), H, axis=1)
    w = (1.0 - p) * MAXD + p * f64(dis)[:, idx]
    return 1.0 / w

@@ -1,0 +1,78 @@
+import concourse.mybir as mybir
+
+F32 = mybir.dt.float32
+U16 = mybir.dt.uint16
+MULT = mybir.AluOpType.mult
+ADD = mybir.AluOpType.add
+SQUARE = mybir.ActivationFunctionType.Square
+ABS_RSQRT = mybir.ActivationFunctionType.Abs_reciprocal_sqrt
+
+P = 128
+POSITIONS = 512
+COLUMNS = 512
+IMAGES = 4
+POINTS = 256
+BLOCKS = POSITIONS // P
+MAX_DISTANCE = 2.0
+PAIR = 2
+PIECE = PAIR * POINTS
+PIECE_LIST_COLUMNS = PIECE // 16
+PIECES = BLOCKS * IMAGES // PAIR
+
+
+def tile_weightedhausdorffdistance_kernel(tc, dis, prob, offs, out):
+    nc = tc.nc
+    dis_blocks = dis.rearrange("(p k) s -> k p s", k=BLOCKS)
+    out_blocks = out.rearrange("(p k) n -> k p n", k=BLOCKS)
+
+    with (
+        tc.tile_pool(name="held", bufs=1) as held,
+        tc.tile_pool(name="work", bufs=4) as work,
+        tc.tile_pool(name="results", bufs=PIECES) as results,
+    ):
+        offsets = held.tile([P, IMAGES * POINTS // 16], U16, name="offsets")
+        nc.sync.dma_start(offsets[:], offs)
+
+        weight = held.tile([P, BLOCKS * IMAGES], F32, name="weight")
+        nc.scalar.dma_start(weight[:], prob.rearrange("(p k) b -> p (k b)", k=BLOCKS))
+
+        windows = []
+        for k in range(BLOCKS):
+            window = held.tile([P, COLUMNS], F32, name=f"window{k}")
+            queue = nc.sync if k % 2 == 0 else nc.scalar
+            queue.dma_start(window[:], dis_blocks[k, :, :])
+            windows.append(window)
+
+        far = held.tile([P, BLOCKS * IMAGES], F32, name="far")
+        nc.vector.tensor_scalar(far[:], weight[:], -MAX_DISTANCE, MAX_DISTANCE, MULT, ADD)
+
+        for k in range(BLOCKS):
+            spread = held.tile([P, IMAGES * POINTS], F32, name=f"spread{k}")
+            nc.vector.tensor_copy(
+                spread[:].rearrange("p (b h) -> p b h", b=IMAGES),
+                weight[:, k * IMAGES : (k + 1) * IMAGES]
+                .unsqueeze(2)
+                .to_broadcast([P, IMAGES, POINTS]),
+            )
+            for half in range(IMAGES // PAIR):
+                picked = windows[k][:].indirect(
+                    offsets[:, half * PIECE_LIST_COLUMNS : (half + 1) * PIECE_LIST_COLUMNS]
+                )
+                near = work.tile([P, PIECE], F32, name="near")
+                nc.vector.tensor_tensor(
+                    near[:], picked, spread[:, half * PIECE : (half + 1) * PIECE], MULT
+                )
+                squared = work.tile([P, PIECE], F32, name="squared")
+                for i in range(PAIR):
+                    column = k * IMAGES + half * PAIR + i
+                    nc.scalar.activation(
+                        squared[:, i * POINTS : (i + 1) * POINTS],
+                        near[:, i * POINTS : (i + 1) * POINTS],
+                        SQUARE,
+                        bias=far[:, column : column + 1],
+                    )
+                inverse = results.tile([P, PIECE], F32, name="inverse")
+                nc.scalar.activation(inverse[:], squared[:], ABS_RSQRT)
+                nc.sync.dma_start(
+                    out_blocks[k, :, half * PIECE : (half + 1) * PIECE], inverse[:]
+                )

@@ -3,7 +3,7 @@ import concourse.mybir as mybir
 F32 = mybir.dt.float32
 U16 = mybir.dt.uint16
 MULT = mybir.AluOpType.mult
-ADD = mybir.AluOpType.add
+COPY = mybir.ActivationFunctionType.Copy
 SQUARE = mybir.ActivationFunctionType.Square
 ABS_RSQRT = mybir.ActivationFunctionType.Abs_reciprocal_sqrt
 
@@ -44,23 +44,31 @@ def tile_weightedhausdorffdistance_kernel(tc, dis, prob, offs, out):
             windows.append(window)
 
         far = held.tile([P, BLOCKS * IMAGES], F32, name="far")
-        nc.vector.tensor_scalar(far[:], weight[:], -MAX_DISTANCE, MAX_DISTANCE, MULT, ADD)
+        nc.scalar.activation(far[:], weight[:], COPY, bias=MAX_DISTANCE, scale=-MAX_DISTANCE)
 
-        for k in range(BLOCKS):
-            spread = held.tile([P, IMAGES * POINTS], F32, name=f"spread{k}")
-            nc.vector.tensor_copy(
-                spread[:].rearrange("p (b h) -> p b h", b=IMAGES),
+        spreads = [
+            held.tile([P, IMAGES * POINTS], F32, name=f"spread{k}") for k in range(BLOCKS)
+        ]
+
+        def spread_weights(k):
+            copy = nc.vector.tensor_copy if k % 2 == 0 else nc.scalar.copy
+            copy(
+                spreads[k][:].rearrange("p (b h) -> p b h", b=IMAGES),
                 weight[:, k * IMAGES : (k + 1) * IMAGES]
                 .unsqueeze(2)
                 .to_broadcast([P, IMAGES, POINTS]),
             )
+
+        spread_weights(0)
+        spread_weights(1)
+        for k in range(BLOCKS):
             for half in range(IMAGES // PAIR):
                 picked = windows[k][:].indirect(
                     offsets[:, half * PIECE_LIST_COLUMNS : (half + 1) * PIECE_LIST_COLUMNS]
                 )
                 near = work.tile([P, PIECE], F32, name="near")
                 nc.vector.tensor_tensor(
-                    near[:], picked, spread[:, half * PIECE : (half + 1) * PIECE], MULT
+                    near[:], picked, spreads[k][:, half * PIECE : (half + 1) * PIECE], MULT
                 )
                 squared = work.tile([P, PIECE], F32, name="squared")
                 for i in range(PAIR):
@@ -76,3 +84,5 @@ def tile_weightedhausdorffdistance_kernel(tc, dis, prob, offs, out):
                 nc.sync.dma_start(
                     out_blocks[k, :, half * PIECE : (half + 1) * PIECE], inverse[:]
                 )
+            if k + 2 < BLOCKS:
+                spread_weights(k + 2)

@@ -50,8 +50,7 @@ def tile_weightedhausdorffdistance_kernel(tc, dis, prob, offs, out):
             held.tile([P, IMAGES * POINTS], F32, name=f"spread{k}") for k in range(BLOCKS)
         ]
 
-        def spread_weights(k):
-            copy = nc.vector.tensor_copy if k % 2 == 0 else nc.scalar.copy
+        def spread_weights(copy, k):
             copy(
                 spreads[k][:].rearrange("p (b h) -> p b h", b=IMAGES),
                 weight[:, k * IMAGES : (k + 1) * IMAGES]
@@ -59,9 +58,11 @@ def tile_weightedhausdorffdistance_kernel(tc, dis, prob, offs, out):
                 .to_broadcast([P, IMAGES, POINTS]),
             )
 
-        spread_weights(0)
-        spread_weights(1)
+        spread_weights(nc.scalar.copy, 1)
+
         for k in range(BLOCKS):
+            if k != 1:
+                spread_weights(nc.vector.tensor_copy, k)
             for half in range(IMAGES // PAIR):
                 picked = windows[k][:].indirect(
                     offsets[:, half * PIECE_LIST_COLUMNS : (half + 1) * PIECE_LIST_COLUMNS]
@@ -84,5 +85,3 @@ def tile_weightedhausdorffdistance_kernel(tc, dis, prob, offs, out):
                 nc.sync.dma_start(
                     out_blocks[k, :, half * PIECE : (half + 1) * PIECE], inverse[:]
                 )
-            if k + 2 < BLOCKS:
-                spread_weights(k + 2)

@@ -3,7 +3,7 @@ import concourse.mybir as mybir
 F32 = mybir.dt.float32
 U16 = mybir.dt.uint16
 MULT = mybir.AluOpType.mult
-COPY = mybir.ActivationFunctionType.Copy
+ADD = mybir.AluOpType.add
 SQUARE = mybir.ActivationFunctionType.Square
 ABS_RSQRT = mybir.ActivationFunctionType.Abs_reciprocal_sqrt
 
@@ -44,44 +44,35 @@ def tile_weightedhausdorffdistance_kernel(tc, dis, prob, offs, out):
             windows.append(window)
 
         far = held.tile([P, BLOCKS * IMAGES], F32, name="far")
-        nc.scalar.activation(far[:], weight[:], COPY, bias=MAX_DISTANCE, scale=-MAX_DISTANCE)
+        nc.vector.tensor_scalar(far[:], weight[:], -MAX_DISTANCE, MAX_DISTANCE, MULT, ADD)
 
-        spreads = [
-            held.tile([P, IMAGES * POINTS], F32, name=f"spread{k}") for k in range(BLOCKS)
-        ]
-
-        def spread_weights(copy, k):
-            copy(
-                spreads[k][:].rearrange("p (b h) -> p b h", b=IMAGES),
+        for k in range(BLOCKS):
+            spread = held.tile([P, IMAGES * POINTS], F32, name=f"spread{k}")
+            nc.vector.tensor_copy(
+                spread[:].rearrange("p (b h) -> p b h", b=IMAGES),
                 weight[:, k * IMAGES : (k + 1) * IMAGES]
                 .unsqueeze(2)
                 .to_broadcast([P, IMAGES, POINTS]),
             )
-
-        spread_weights(nc.scalar.copy, 1)
-
-        for k in range(BLOCKS):
-            if k != 1:
-                spread_weights(nc.vector.tensor_copy, k)
             for half in range(IMAGES // PAIR):
                 picked = windows[k][:].indirect(
                     offsets[:, half * PIECE_LIST_COLUMNS : (half + 1) * PIECE_LIST_COLUMNS]
                 )
                 near = work.tile([P, PIECE], F32, name="near")
                 nc.vector.tensor_tensor(
-                    near[:], picked, spreads[k][:, half * PIECE : (half + 1) * PIECE], MULT
+                    near[:], picked, spread[:, half * PIECE : (half + 1) * PIECE], MULT
                 )
-                squared = work.tile([P, PIECE], F32, name="squared")
+                root = work.tile([P, PIECE], F32, name="root")
                 for i in range(PAIR):
                     column = k * IMAGES + half * PAIR + i
                     nc.scalar.activation(
-                        squared[:, i * POINTS : (i + 1) * POINTS],
+                        root[:, i * POINTS : (i + 1) * POINTS],
                         near[:, i * POINTS : (i + 1) * POINTS],
-                        SQUARE,
+                        ABS_RSQRT,
                         bias=far[:, column : column + 1],
                     )
                 inverse = results.tile([P, PIECE], F32, name="inverse")
-                nc.scalar.activation(inverse[:], squared[:], ABS_RSQRT)
+                nc.scalar.activation(inverse[:], root[:], SQUARE)
                 nc.sync.dma_start(
                     out_blocks[k, :, half * PIECE : (half + 1) * PIECE], inverse[:]
                 )

@@ -17,7 +17,6 @@ MAX_DISTANCE = 2.0
 PAIR = 2
 PIECE = PAIR * POINTS
 PIECE_LIST_COLUMNS = PIECE // 16
-PIECES = BLOCKS * IMAGES // PAIR
 
 
 def tile_weightedhausdorffdistance_kernel(tc, dis, prob, offs, out):
@@ -28,7 +27,7 @@ def tile_weightedhausdorffdistance_kernel(tc, dis, prob, offs, out):
     with (
         tc.tile_pool(name="held", bufs=1) as held,
         tc.tile_pool(name="work", bufs=4) as work,
-        tc.tile_pool(name="results", bufs=PIECES) as results,
+        tc.tile_pool(name="results", bufs=BLOCKS * IMAGES) as results,
     ):
         offsets = held.tile([P, IMAGES * POINTS // 16], U16, name="offsets")
         nc.sync.dma_start(offsets[:], offs)
@@ -71,8 +70,12 @@ def tile_weightedhausdorffdistance_kernel(tc, dis, prob, offs, out):
                         ABS_RSQRT,
                         bias=far[:, column : column + 1],
                     )
-                inverse = results.tile([P, PIECE], F32, name="inverse")
-                nc.scalar.activation(inverse[:], root[:], SQUARE)
-                nc.sync.dma_start(
-                    out_blocks[k, :, half * PIECE : (half + 1) * PIECE], inverse[:]
-                )
+                for i in range(PAIR):
+                    b = half * PAIR + i
+                    inverse = results.tile([P, POINTS], F32, name="inverse")
+                    nc.scalar.activation(
+                        inverse[:], root[:, i * POINTS : (i + 1) * POINTS], SQUARE
+                    )
+                    nc.sync.dma_start(
+                        out_blocks[k, :, b * POINTS : (b + 1) * POINTS], inverse[:]
+                    )

@@ -3,7 +3,7 @@ import concourse.mybir as mybir
 F32 = mybir.dt.float32
 U16 = mybir.dt.uint16
 MULT = mybir.AluOpType.mult
-ADD = mybir.AluOpType.add
+COPY = mybir.ActivationFunctionType.Copy
 SQUARE = mybir.ActivationFunctionType.Square
 ABS_RSQRT = mybir.ActivationFunctionType.Abs_reciprocal_sqrt
 
@@ -42,24 +42,33 @@ def tile_weightedhausdorffdistance_kernel(tc, dis, prob, offs, out):
             queue.dma_start(window[:], dis_blocks[k, :, :])
             windows.append(window)
 
-        far = held.tile([P, BLOCKS * IMAGES], F32, name="far")
-        nc.vector.tensor_scalar(far[:], weight[:], -MAX_DISTANCE, MAX_DISTANCE, MULT, ADD)
+        primer = held.tile([P, 1], F32, name="primer")
+        nc.gpsimd.memset(primer[:], 1.0)
+        nc.scalar.activation(primer[:], primer[:], ABS_RSQRT)
 
+        far = held.tile([P, BLOCKS * IMAGES], F32, name="far")
+        nc.scalar.activation(far[:], weight[:], COPY, bias=MAX_DISTANCE, scale=-MAX_DISTANCE)
+
+        spreads = []
         for k in range(BLOCKS):
             spread = held.tile([P, IMAGES * POINTS], F32, name=f"spread{k}")
-            nc.vector.tensor_copy(
+            copy = nc.vector.tensor_copy if k < BLOCKS // 2 else nc.scalar.copy
+            copy(
                 spread[:].rearrange("p (b h) -> p b h", b=IMAGES),
                 weight[:, k * IMAGES : (k + 1) * IMAGES]
                 .unsqueeze(2)
                 .to_broadcast([P, IMAGES, POINTS]),
             )
+            spreads.append(spread)
+
+        for k in range(BLOCKS):
             for half in range(IMAGES // PAIR):
                 picked = windows[k][:].indirect(
                     offsets[:, half * PIECE_LIST_COLUMNS : (half + 1) * PIECE_LIST_COLUMNS]
                 )
                 near = work.tile([P, PIECE], F32, name="near")
                 nc.vector.tensor_tensor(
-                    near[:], picked, spread[:, half * PIECE : (half + 1) * PIECE], MULT
+                    near[:], picked, spreads[k][:, half * PIECE : (half + 1) * PIECE], MULT
                 )
                 root = work.tile([P, PIECE], F32, name="root")
                 for i in range(PAIR):

@@ -15,8 +15,7 @@ POINTS = 256
 BLOCKS = POSITIONS // P
 MAX_DISTANCE = 2.0
 PAIR = 2
-PIECE = PAIR * POINTS
-PIECE_LIST_COLUMNS = PIECE // 16
+LIST_COLUMNS = POINTS // 16
 
 
 def tile_weightedhausdorffdistance_kernel(tc, dis, prob, offs, out):
@@ -61,30 +60,31 @@ def tile_weightedhausdorffdistance_kernel(tc, dis, prob, offs, out):
             )
             spreads.append(spread)
 
-        for k in range(BLOCKS):
-            for half in range(IMAGES // PAIR):
-                picked = windows[k][:].indirect(
-                    offsets[:, half * PIECE_LIST_COLUMNS : (half + 1) * PIECE_LIST_COLUMNS]
+        pieces = [(k, first, PAIR) for k in range(BLOCKS) for first in range(0, IMAGES, PAIR)]
+        k, first, count = pieces.pop()
+        pieces.extend((k, first + i, 1) for i in range(count))
+
+        for k, first, count in pieces:
+            images = range(first, first + count)
+            picked = windows[k][:].indirect(
+                offsets[:, first * LIST_COLUMNS : (first + count) * LIST_COLUMNS]
+            )
+            near = work.tile([P, PAIR * POINTS], F32, name="near")
+            nc.vector.tensor_tensor(
+                near[:, : count * POINTS],
+                picked,
+                spreads[k][:, first * POINTS : (first + count) * POINTS],
+                MULT,
+            )
+            root = work.tile([P, PAIR * POINTS], F32, name="root")
+            for i, b in enumerate(images):
+                nc.scalar.activation(
+                    root[:, i * POINTS : (i + 1) * POINTS],
+                    near[:, i * POINTS : (i + 1) * POINTS],
+                    ABS_RSQRT,
+                    bias=far[:, k * IMAGES + b : k * IMAGES + b + 1],
                 )
-                near = work.tile([P, PIECE], F32, name="near")
-                nc.vector.tensor_tensor(
-                    near[:], picked, spreads[k][:, half * PIECE : (half + 1) * PIECE], MULT
-                )
-                root = work.tile([P, PIECE], F32, name="root")
-                for i in range(PAIR):
-                    column = k * IMAGES + half * PAIR + i
-                    nc.scalar.activation(
-                        root[:, i * POINTS : (i + 1) * POINTS],
-                        near[:, i * POINTS : (i + 1) * POINTS],
-                        ABS_RSQRT,
-                        bias=far[:, column : column + 1],
-                    )
-                for i in range(PAIR):
-                    b = half * PAIR + i
-                    inverse = results.tile([P, POINTS], F32, name="inverse")
-                    nc.scalar.activation(
-                        inverse[:], root[:, i * POINTS : (i + 1) * POINTS], SQUARE
-                    )
-                    nc.sync.dma_start(
-                        out_blocks[k, :, b * POINTS : (b + 1) * POINTS], inverse[:]
-                    )
+            for i, b in enumerate(images):
+                inverse = results.tile([P, POINTS], F32, name="inverse")
+                nc.scalar.activation(inverse[:], root[:, i * POINTS : (i + 1) * POINTS], SQUARE)
+                nc.sync.dma_start(out_blocks[k, :, b * POINTS : (b + 1) * POINTS], inverse[:])

@@ -14,7 +14,6 @@ IMAGES = 4
 POINTS = 256
 BLOCKS = POSITIONS // P
 MAX_DISTANCE = 2.0
-PAIR = 2
 LIST_COLUMNS = POINTS // 16
 
 
@@ -60,31 +59,29 @@ def tile_weightedhausdorffdistance_kernel(tc, dis, prob, offs, out):
             )
             spreads.append(spread)
 
-        pieces = [(k, first, PAIR) for k in range(BLOCKS) for first in range(0, IMAGES, PAIR)]
-        k, first, count = pieces.pop()
-        pieces.extend((k, first + i, 1) for i in range(count))
+        def square_and_store(k, b, root):
+            inverse = results.tile([P, POINTS], F32, name="inverse")
+            nc.scalar.activation(inverse[:], root[:], SQUARE)
+            nc.sync.dma_start(out_blocks[k, :, b * POINTS : (b + 1) * POINTS], inverse[:])
 
-        for k, first, count in pieces:
-            images = range(first, first + count)
-            picked = windows[k][:].indirect(
-                offsets[:, first * LIST_COLUMNS : (first + count) * LIST_COLUMNS]
-            )
-            near = work.tile([P, PAIR * POINTS], F32, name="near")
-            nc.vector.tensor_tensor(
-                near[:, : count * POINTS],
-                picked,
-                spreads[k][:, first * POINTS : (first + count) * POINTS],
-                MULT,
-            )
-            root = work.tile([P, PAIR * POINTS], F32, name="root")
-            for i, b in enumerate(images):
+        waiting = None
+        for k in range(BLOCKS):
+            for b in range(IMAGES):
+                near = work.tile([P, POINTS], F32, name="near")
+                nc.vector.tensor_tensor(
+                    near[:],
+                    windows[k][:].indirect(offsets[:, b * LIST_COLUMNS : (b + 1) * LIST_COLUMNS]),
+                    spreads[k][:, b * POINTS : (b + 1) * POINTS],
+                    MULT,
+                )
+                root = work.tile([P, POINTS], F32, name="root")
                 nc.scalar.activation(
-                    root[:, i * POINTS : (i + 1) * POINTS],
-                    near[:, i * POINTS : (i + 1) * POINTS],
+                    root[:],
+                    near[:],
                     ABS_RSQRT,
                     bias=far[:, k * IMAGES + b : k * IMAGES + b + 1],
                 )
-            for i, b in enumerate(images):
-                inverse = results.tile([P, POINTS], F32, name="inverse")
-                nc.scalar.activation(inverse[:], root[:, i * POINTS : (i + 1) * POINTS], SQUARE)
-                nc.sync.dma_start(out_blocks[k, :, b * POINTS : (b + 1) * POINTS], inverse[:])
+                if waiting is not None:
+                    square_and_store(*waiting)
+                waiting = (k, b, root)
+        square_and_store(*waiting)

@@ -27,22 +27,21 @@ def tile_weightedhausdorffdistance_kernel(tc, dis, prob, offs, out):
         tc.tile_pool(name="work", bufs=4) as work,
         tc.tile_pool(name="results", bufs=BLOCKS * IMAGES) as results,
     ):
-        offsets = held.tile([P, IMAGES * POINTS // 16], U16, name="offsets")
-        nc.sync.dma_start(offsets[:], offs)
+        primer = held.tile([P, 1], F32, name="primer")
+        nc.vector.memset(primer[:], 1.0)
+        nc.scalar.activation(primer[:], primer[:], ABS_RSQRT)
 
         weight = held.tile([P, BLOCKS * IMAGES], F32, name="weight")
-        nc.scalar.dma_start(weight[:], prob.rearrange("(p k) b -> p (k b)", k=BLOCKS))
+        nc.sync.dma_start(weight[:], prob.rearrange("(p k) b -> p (k b)", k=BLOCKS))
+
+        offsets = held.tile([P, IMAGES * POINTS // 16], U16, name="offsets")
+        nc.sync.dma_start(offsets[:], offs)
 
         windows = []
         for k in range(BLOCKS):
             window = held.tile([P, COLUMNS], F32, name=f"window{k}")
-            queue = nc.sync if k % 2 == 0 else nc.scalar
-            queue.dma_start(window[:], dis_blocks[k, :, :])
+            nc.sync.dma_start(window[:], dis_blocks[k, :, :])
             windows.append(window)
-
-        primer = held.tile([P, 1], F32, name="primer")
-        nc.gpsimd.memset(primer[:], 1.0)
-        nc.scalar.activation(primer[:], primer[:], ABS_RSQRT)
 
         far = held.tile([P, BLOCKS * IMAGES], F32, name="far")
         nc.scalar.activation(far[:], weight[:], COPY, bias=MAX_DISTANCE, scale=-MAX_DISTANCE)

@@ -24,8 +24,7 @@ def tile_weightedhausdorffdistance_kernel(tc, dis, prob, offs, out):
 
     with (
         tc.tile_pool(name="held", bufs=1) as held,
-        tc.tile_pool(name="work", bufs=4) as work,
-        tc.tile_pool(name="results", bufs=BLOCKS * IMAGES) as results,
+        tc.tile_pool(name="work", bufs=BLOCKS * IMAGES) as work,
     ):
         primer = held.tile([P, 1], F32, name="primer")
         nc.vector.memset(primer[:], 1.0)
@@ -58,29 +57,44 @@ def tile_weightedhausdorffdistance_kernel(tc, dis, prob, offs, out):
             )
             spreads.append(spread)
 
-        def square_and_store(k, b, root):
-            inverse = results.tile([P, POINTS], F32, name="inverse")
-            nc.scalar.activation(inverse[:], root[:], SQUARE)
+        def look_up(k, b):
+            near = work.tile([P, POINTS], F32, name="near")
+            nc.vector.tensor_tensor(
+                near[:],
+                windows[k][:].indirect(offsets[:, b * LIST_COLUMNS : (b + 1) * LIST_COLUMNS]),
+                spreads[k][:, b * POINTS : (b + 1) * POINTS],
+                MULT,
+            )
+            return near
+
+        def take_root(k, b, root, near):
+            bias = far[:, k * IMAGES + b : k * IMAGES + b + 1]
+            nc.scalar.activation(root, near, ABS_RSQRT, bias=bias)
+
+        def store(k, b, inverse):
             nc.sync.dma_start(out_blocks[k, :, b * POINTS : (b + 1) * POINTS], inverse[:])
 
+        *pieces, last = [(k, b) for k in range(BLOCKS) for b in range(IMAGES)]
         waiting = None
-        for k in range(BLOCKS):
-            for b in range(IMAGES):
-                near = work.tile([P, POINTS], F32, name="near")
-                nc.vector.tensor_tensor(
-                    near[:],
-                    windows[k][:].indirect(offsets[:, b * LIST_COLUMNS : (b + 1) * LIST_COLUMNS]),
-                    spreads[k][:, b * POINTS : (b + 1) * POINTS],
-                    MULT,
-                )
-                root = work.tile([P, POINTS], F32, name="root")
-                nc.scalar.activation(
-                    root[:],
-                    near[:],
-                    ABS_RSQRT,
-                    bias=far[:, k * IMAGES + b : k * IMAGES + b + 1],
-                )
-                if waiting is not None:
-                    square_and_store(*waiting)
-                waiting = (k, b, root)
-        square_and_store(*waiting)
+        for k, b in pieces:
+            near = look_up(k, b)
+            root = work.tile([P, POINTS], F32, name="root")
+            take_root(k, b, root[:], near[:])
+            if waiting is not None:
+                inverse = work.tile([P, POINTS], F32, name="inverse")
+                nc.scalar.activation(inverse[:], waiting[2][:], SQUARE)
+                store(waiting[0], waiting[1], inverse)
+            waiting = (k, b, root)
+
+        near = look_up(*last)
+        inverse = work.tile([P, POINTS], F32, name="inverse")
+        nc.vector.tensor_tensor(inverse[:], waiting[2][:], waiting[2][:], MULT)
+        store(waiting[0], waiting[1], inverse)
+        root = work.tile([P, POINTS], F32, name="root")
+        inverse = work.tile([P, POINTS], F32, name="inverse")
+        halves = (slice(0, POINTS // 2), slice(POINTS // 2, POINTS))
+        for half in halves:
+            take_root(*last, root[:, half], near[:, half])
+        for half in halves:
+            nc.scalar.activation(inverse[:, half], root[:, half], SQUARE)
+        store(*last, inverse)

@@ -13,6 +13,7 @@ COLUMNS = 512
 IMAGES = 4
 POINTS = 256
 BLOCKS = POSITIONS // P
+PAIR = 2
 MAX_DISTANCE = 2.0
 LIST_COLUMNS = POINTS // 16
 
@@ -33,14 +34,12 @@ def tile_weightedhausdorffdistance_kernel(tc, dis, prob, offs, out):
         weight = held.tile([P, BLOCKS * IMAGES], F32, name="weight")
         nc.sync.dma_start(weight[:], prob.rearrange("(p k) b -> p (k b)", k=BLOCKS))
 
+        windows = [held.tile([P, COLUMNS], F32, name=f"window{k}") for k in range(BLOCKS)]
         offsets = held.tile([P, IMAGES * POINTS // 16], U16, name="offsets")
+        nc.sync.dma_start(windows[0][:], dis_blocks[0, :, :])
         nc.sync.dma_start(offsets[:], offs)
-
-        windows = []
-        for k in range(BLOCKS):
-            window = held.tile([P, COLUMNS], F32, name=f"window{k}")
-            nc.sync.dma_start(window[:], dis_blocks[k, :, :])
-            windows.append(window)
+        for k in range(1, BLOCKS):
+            nc.sync.dma_start(windows[k][:], dis_blocks[k, :, :])
 
         far = held.tile([P, BLOCKS * IMAGES], F32, name="far")
         nc.scalar.activation(far[:], weight[:], COPY, bias=MAX_DISTANCE, scale=-MAX_DISTANCE)
@@ -71,8 +70,9 @@ def tile_weightedhausdorffdistance_kernel(tc, dis, prob, offs, out):
             bias = far[:, k * IMAGES + b : k * IMAGES + b + 1]
             nc.scalar.activation(root, near, ABS_RSQRT, bias=bias)
 
-        def store(k, b, inverse):
-            nc.sync.dma_start(out_blocks[k, :, b * POINTS : (b + 1) * POINTS], inverse[:])
+        def store(k, first, images, inverse):
+            columns = slice(first * POINTS, (first + images) * POINTS)
+            nc.sync.dma_start(out_blocks[k, :, columns], inverse[:])
 
         *pieces, last = [(k, b) for k in range(BLOCKS) for b in range(IMAGES)]
         waiting = None
@@ -81,20 +81,27 @@ def tile_weightedhausdorffdistance_kernel(tc, dis, prob, offs, out):
             root = work.tile([P, POINTS], F32, name="root")
             take_root(k, b, root[:], near[:])
             if waiting is not None:
-                inverse = work.tile([P, POINTS], F32, name="inverse")
-                nc.scalar.activation(inverse[:], waiting[2][:], SQUARE)
-                store(waiting[0], waiting[1], inverse)
+                ready_k, ready_b, ready_root = waiting
+                images = 1 if ready_k == BLOCKS - 1 else PAIR
+                place = ready_b % images
+                if place == 0:
+                    inverse = work.tile([P, images * POINTS], F32, name=f"inverse{images}")
+                square = inverse[:, place * POINTS : (place + 1) * POINTS]
+                nc.scalar.activation(square, ready_root[:], SQUARE)
+                if place == images - 1:
+                    store(ready_k, ready_b - place, images, inverse)
             waiting = (k, b, root)
 
         near = look_up(*last)
-        inverse = work.tile([P, POINTS], F32, name="inverse")
-        nc.vector.tensor_tensor(inverse[:], waiting[2][:], waiting[2][:], MULT)
-        store(waiting[0], waiting[1], inverse)
+        k, b, root = waiting
+        inverse = work.tile([P, POINTS], F32, name="inverse1")
+        nc.vector.tensor_tensor(inverse[:], root[:], root[:], MULT)
+        store(k, b, 1, inverse)
         root = work.tile([P, POINTS], F32, name="root")
-        inverse = work.tile([P, POINTS], F32, name="inverse")
+        inverse = work.tile([P, POINTS], F32, name="inverse1")
         halves = (slice(0, POINTS // 2), slice(POINTS // 2, POINTS))
         for half in halves:
             take_root(*last, root[:, half], near[:, half])
         for half in halves:
             nc.scalar.activation(inverse[:, half], root[:, half], SQUARE)
-        store(*last, inverse)
+        store(*last, 1, inverse)

import concourse.mybir as mybir

F32 = mybir.dt.float32
U16 = mybir.dt.uint16
MULT = mybir.AluOpType.mult
COPY = mybir.ActivationFunctionType.Copy
SQUARE = mybir.ActivationFunctionType.Square
ABS_RSQRT = mybir.ActivationFunctionType.Abs_reciprocal_sqrt

P = 128
POSITIONS = 512
COLUMNS = 512
IMAGES = 4
POINTS = 256
BLOCKS = POSITIONS // P
PAIR = 2
MAX_DISTANCE = 2.0
LIST_COLUMNS = POINTS // 16


def tile_weightedhausdorffdistance_kernel(tc, dis, prob, offs, out):
    nc = tc.nc
    dis_blocks = dis.rearrange("(p k) s -> k p s", k=BLOCKS)
    out_blocks = out.rearrange("(p k) n -> k p n", k=BLOCKS)

    with (
        tc.tile_pool(name="held", bufs=1) as held,
        tc.tile_pool(name="work", bufs=BLOCKS * IMAGES) as work,
    ):
        primer = held.tile([P, 1], F32, name="primer")
        nc.vector.memset(primer[:], 1.0)
        nc.scalar.activation(primer[:], primer[:], ABS_RSQRT)

        weight = held.tile([P, BLOCKS * IMAGES], F32, name="weight")
        nc.sync.dma_start(weight[:], prob.rearrange("(p k) b -> p (k b)", k=BLOCKS))

        windows = [held.tile([P, COLUMNS], F32, name=f"window{k}") for k in range(BLOCKS)]
        offsets = held.tile([P, IMAGES * POINTS // 16], U16, name="offsets")
        nc.sync.dma_start(windows[0][:], dis_blocks[0, :, :])
        nc.sync.dma_start(offsets[:], offs)
        for k in range(1, BLOCKS):
            nc.sync.dma_start(windows[k][:], dis_blocks[k, :, :])

        far = held.tile([P, BLOCKS * IMAGES], F32, name="far")
        nc.scalar.activation(far[:], weight[:], COPY, bias=MAX_DISTANCE, scale=-MAX_DISTANCE)

        spreads = []
        for k in range(BLOCKS):
            spread = held.tile([P, IMAGES * POINTS], F32, name=f"spread{k}")
            copy = nc.vector.tensor_copy if k < BLOCKS // 2 else nc.scalar.copy
            copy(
                spread[:].rearrange("p (b h) -> p b h", b=IMAGES),
                weight[:, k * IMAGES : (k + 1) * IMAGES]
                .unsqueeze(2)
                .to_broadcast([P, IMAGES, POINTS]),
            )
            spreads.append(spread)

        def look_up(k, b):
            near = work.tile([P, POINTS], F32, name="near")
            nc.vector.tensor_tensor(
                near[:],
                windows[k][:].indirect(offsets[:, b * LIST_COLUMNS : (b + 1) * LIST_COLUMNS]),
                spreads[k][:, b * POINTS : (b + 1) * POINTS],
                MULT,
            )
            return near

        def take_root(k, b, root, near):
            bias = far[:, k * IMAGES + b : k * IMAGES + b + 1]
            nc.scalar.activation(root, near, ABS_RSQRT, bias=bias)

        def store(k, first, images, inverse):
            columns = slice(first * POINTS, (first + images) * POINTS)
            nc.sync.dma_start(out_blocks[k, :, columns], inverse[:])

        *pieces, last = [(k, b) for k in range(BLOCKS) for b in range(IMAGES)]
        waiting = None
        for k, b in pieces:
            near = look_up(k, b)
            root = work.tile([P, POINTS], F32, name="root")
            take_root(k, b, root[:], near[:])
            if waiting is not None:
                ready_k, ready_b, ready_root = waiting
                images = 1 if ready_k == BLOCKS - 1 else PAIR
                place = ready_b % images
                if place == 0:
                    inverse = work.tile([P, images * POINTS], F32, name=f"inverse{images}")
                square = inverse[:, place * POINTS : (place + 1) * POINTS]
                nc.scalar.activation(square, ready_root[:], SQUARE)
                if place == images - 1:
                    store(ready_k, ready_b - place, images, inverse)
            waiting = (k, b, root)

        near = look_up(*last)
        k, b, root = waiting
        inverse = work.tile([P, POINTS], F32, name="inverse1")
        nc.vector.tensor_tensor(inverse[:], root[:], root[:], MULT)
        store(k, b, 1, inverse)
        root = work.tile([P, POINTS], F32, name="root")
        inverse = work.tile([P, POINTS], F32, name="inverse1")
        halves = (slice(0, POINTS // 2), slice(POINTS // 2, POINTS))
        for half in halves:
            take_root(*last, root[:, half], near[:, half])
        for half in halves:
            nc.scalar.activation(inverse[:, half], root[:, half], SQUARE)
        store(*last, 1, inverse)
